import numpy as np
import ml_dtypes


def mxq(x, axis, fmt="e4m3"):
    dtype, down = {"e4m3": (ml_dtypes.float8_e4m3fn, 7), "e5m2": (ml_dtypes.float8_e5m2, 14)}[fmt]
    v = np.moveaxis(np.asarray(x, np.float32).astype(ml_dtypes.bfloat16).astype(np.float64), axis, -1)
    blocks = v.reshape(v.shape[:-1] + (-1, 32))
    amax = np.abs(blocks).max(-1, keepdims=True)
    byte = np.maximum(np.where(amax > 0, np.frexp(amax)[1] - 1 + 127, 0) - down, 1)
    scale = np.exp2(byte - 127.0)
    codes = (blocks / scale).astype(np.float32).astype(dtype).astype(np.float64)
    return np.moveaxis((codes * scale).reshape(v.shape), -1, axis)


WIDE = False


def mx_kscale(k):
    if not WIDE:
        return np.ones(k)
    levels = np.array([10, -10, 5, -5, 0])
    a = np.random.permutation(np.resize(levels, k // 512 * 4)).reshape(k // 512, 4)
    idx = np.arange(k)
    return np.exp2(a[idx // 512, idx % 128 // 32])


BF16 = ml_dtypes.bfloat16


def bf(x):
    return np.asarray(x, np.float32).astype(BF16)


def f64(x):
    return np.asarray(x).astype(np.float64)


E2M1 = np.array([0.0, 0.5, 1.0, 1.5, 2.0, 3.0, 4.0, 6.0, -0.0, -0.5, -1.0, -1.5, -2.0, -3.0, -4.0, -6.0])


def pack_weight(w, fmt):
    k, n = w.shape
    w = f64(bf(w)).reshape(k // 32, 32, n)
    amax = np.abs(w).max(1)
    if fmt == "e4m3":
        byte = np.frexp(amax)[1] - 1 + 127 - 7
    else:
        mant, ex = np.frexp(amax / 6.0)
        byte = np.where(mant > 0.5, ex, ex - 1) + 127
    byte = np.clip(np.where(amax > 0, byte, 1), 1, 254)
    scaled = (w * np.exp2(127.0 - byte)[:, None, :]).reshape(k, n).astype(np.float32)
    by_word = np.ascontiguousarray(scaled.reshape(k // 512, 128, 4, n).transpose(0, 1, 3, 2))
    if fmt == "e4m3":
        words = by_word.astype(ml_dtypes.float8_e4m3fn).view(np.uint8)
    else:
        c = by_word.astype(ml_dtypes.float4_e2m1fn).view(np.uint8) & 0xF
        words = c[..., 0::2] | (c[..., 1::2] << 4)
    return np.ascontiguousarray(words), np.ascontiguousarray(byte.astype(np.uint8).reshape(k // 512, 16, n))


def unpack_weight(words, scales, fmt):
    g, p, n, _ = words.shape
    if fmt == "e4m3":
        vals = np.ascontiguousarray(words).view(ml_dtypes.float8_e4m3fn).astype(np.float64)
    else:
        nib = np.empty((g, p, n, 4), np.uint8)
        nib[..., 0::2] = words & 0xF
        nib[..., 1::2] = words >> 4
        vals = E2M1[nib]
    vals = vals * np.repeat(np.exp2(scales.astype(np.float64) - 127.0), 8, axis=1)[..., None]
    return vals.transpose(0, 1, 3, 2).reshape(g * 512, n)

def pack4(w):
    words, scales = pack_weight(w, "e2m1")
    return words.reshape(words.shape[0], 128, -1), scales


def unpack4(words, scales):
    return unpack_weight(words.reshape(words.shape[0], 128, -1, 2), scales, "e2m1")


B, L_IMG, L_TXT, DM, H, D = 1, 128, 128, 512, 8, 64
L = L_TXT + L_IMG
HD = H * D
EPS = 1e-6


def rms(x, gain):
    return x / np.sqrt(np.mean(np.square(x), axis=-1, keepdims=True) + EPS) * gain


def qkv(x, w, qn, kn):
    y = (mxq(x, 2, "e4m3") @ w).reshape(x.shape[0], x.shape[1], 3, H, D)
    return rms(y[:, :, 0], qn), rms(y[:, :, 1], kn), y[:, :, 2]


def rope(x, fc):
    x_ = x.reshape(x.shape[:-1] + (D // 2, 1, 2))
    out = fc[:, None, :, :, 0] * x_[..., 0] + fc[:, None, :, :, 1] * x_[..., 1]
    return out.reshape(x.shape)


def setup_inputs():
    s = mx_kscale(DM)
    r = np.random.standard_normal
    hidden_states = bf(r((B, L_IMG, DM)) * s)
    encoder_hidden_states = bf(r((B, L_TXT, DM)) * s)
    image_rotary_emb = bf(r((L, D // 2, 4)) * 0.6)
    iqkv_words, iqkv_scales = pack4(r((DM, 3 * HD)) / np.sqrt(DM) / s[:, None])
    eqkv_words, eqkv_scales = pack4(r((DM, 3 * HD)) / np.sqrt(DM) / s[:, None])
    return {
        "hidden_states": hidden_states,
        "encoder_hidden_states": encoder_hidden_states,
        "image_rotary_emb": image_rotary_emb,
        "W_iqkv_words": iqkv_words,
        "W_iqkv_scales": iqkv_scales,
        "W_eqkv_words": eqkv_words,
        "W_eqkv_scales": eqkv_scales,
        "qn_scale": bf(1.0 + 0.1 * r(D)),
        "kn_scale": bf(1.0 + 0.1 * r(D)),
        "eqn_scale": bf(1.0 + 0.1 * r(D)),
        "ekn_scale": bf(1.0 + 0.1 * r(D)),
    }


def reference(hidden_states, encoder_hidden_states, image_rotary_emb, W_iqkv_words, W_iqkv_scales, W_eqkv_words, W_eqkv_scales, qn_scale, kn_scale, eqn_scale, ekn_scale):
    q, k, v = qkv(f64(hidden_states), unpack4(W_iqkv_words, W_iqkv_scales), f64(qn_scale), f64(kn_scale))
    eq, ek, ev = qkv(f64(encoder_hidden_states), unpack4(W_eqkv_words, W_eqkv_scales), f64(eqn_scale), f64(ekn_scale))
    q = np.concatenate((eq, q), axis=1)
    k = np.concatenate((ek, k), axis=1)
    v = np.concatenate((ev, v), axis=1)
    fc = f64(image_rotary_emb).reshape(L, D // 2, 2, 2)
    return rope(q, fc).reshape(B, L, HD), rope(k, fc).reshape(B, L, HD), v.reshape(B, L, HD)

@@ -1,0 +1,166 @@
+from contextlib import ExitStack
+
+import concourse.mybir as mybir
+from concourse.masks import make_identity
+
+F32 = mybir.dt.float32
+BF16 = mybir.dt.bfloat16
+I32 = mybir.dt.int32
+U32 = mybir.dt.uint32
+U8 = mybir.dt.uint8
+FP8X4 = mybir.dt.float8_e4m3fn_x4
+FP4X4 = mybir.dt.float4_e2m1fn_x4
+ACT = mybir.ActivationFunctionType
+ALU = mybir.AluOpType
+
+P = 128
+DM = 512
+H = 8
+D = 64
+HD = H * D
+EPS = 1e-6
+STREAMS = 2
+
+FLOPS = 2 * STREAMS * P * DM * 3 * HD
+
+
+def tile_fluxattention_pa_s_kernel(
+    tc,
+    hidden_states,
+    encoder_hidden_states,
+    image_rotary_emb,
+    W_iqkv_words,
+    W_iqkv_scales,
+    W_eqkv_words,
+    W_eqkv_scales,
+    qn_scale,
+    kn_scale,
+    eqn_scale,
+    ekn_scale,
+    out_0,
+    out_1,
+    out_2,
+):
+    nc = tc.nc
+    x_dram = (encoder_hidden_states, hidden_states)
+    words_dram = (W_eqkv_words, W_iqkv_words)
+    scales_dram = (W_eqkv_scales, W_iqkv_scales)
+    gains_dram = ((eqn_scale, ekn_scale), (qn_scale, kn_scale))
+    outs = (out_0, out_1, out_2)
+
+    with ExitStack() as ctx:
+        keep = ctx.enter_context(tc.tile_pool(name="keep", bufs=1))
+        psum = ctx.enter_context(tc.psum_pool(name="psum", bufs=1))
+
+        gain_rows = keep.tile([P, 4 * D], BF16, name="gain_rows")
+        nc.vector.memset(gain_rows[:], 0.0)
+        w_scales = [keep.tile([P, 3 * HD], U8, name="w_scales%d" % s, align_bytes=64) for s in range(STREAMS)]
+        for s in range(STREAMS):
+            nc.vector.memset(w_scales[s][:].bitcast(I32), 0)
+        ones = keep.tile([P, P], BF16, name="ones")
+        nc.vector.memset(ones[:], 1.0)
+        eps = keep.tile([P, 1], F32, name="eps")
+        nc.vector.memset(eps[:], EPS)
+        identity = keep.tile([P, P], F32, name="identity")
+        make_identity(nc, identity[:])
+        warm = keep.tile([P, 1], F32, name="warm")
+        nc.scalar.activation(out=warm[:], in_=eps[:], func=ACT.Abs_reciprocal_sqrt)
+
+        x_sb = [keep.tile([P, DM], BF16, name="x_sb%d" % s) for s in range(STREAMS)]
+        w_words = [keep.tile([P, 2 * 3 * HD], U8, name="w_words%d" % s, align_bytes=64) for s in range(STREAMS)]
+        for s in range(STREAMS):
+            nc.sync.dma_start(out=x_sb[s][:], in_=x_dram[s][0])
+        for s in range(STREAMS):
+            for r in range(4):
+                nc.sync.dma_start(
+                    out=w_scales[s][r:P:32, :].bitcast(I32), in_=scales_dram[s][0, r:16:4, :].bitcast(I32)
+                )
+            nc.sync.dma_start(out=w_words[s][:].bitcast(I32), in_=words_dram[s][0].bitcast(I32))
+        rot = keep.tile([P, STREAMS, 2 * D], BF16, name="rot")
+        nc.scalar.dma_start(out=rot[:], in_=image_rotary_emb.rearrange("(s p) i c -> p s (i c)", s=STREAMS))
+        for s in range(STREAMS):
+            for j in range(2):
+                c = (2 * s + j) * D
+                nc.gpsimd.dma_start(out=gain_rows[0:1, c : c + D], in_=gains_dram[s][j].unsqueeze(0))
+
+        xt = psum.tile([P, STREAMS, 2, P], F32, name="xt")
+        x_codes = []
+        x_scales = []
+        for s in range(STREAMS):
+            for u in range(2):
+                nc.tensor.transpose(xt[:, s, u, :], x_sb[s][:].bitcast(F32)[:, u : DM // 2 : 2], identity[:])
+            grouped = keep.tile([P, 4 * P], BF16, name="grouped%d" % s, align_bytes=64)
+            nc.vector.tensor_copy(
+                out=grouped[:].bitcast(F32).rearrange("p (r u) -> p r u", u=2),
+                in_=xt[:, s].rearrange("p u r -> p r u"),
+            )
+            codes = keep.tile([P, P], U32, name="x_codes%d" % s, align_bytes=64)
+            scales = keep.tile([P, P], U8, name="x_scales%d" % s, align_bytes=64)
+            nc.vector.quantize_mx(out=codes[:].bitcast(FP8X4), scales=scales[:], in_=grouped[:])
+            x_codes.append(codes)
+            x_scales.append(scales)
+
+        gain_all = psum.tile([P, 4 * D], F32, name="gain_all")
+        g = {}
+        for s in range(STREAMS):
+            for j in range(2):
+                c = (2 * s + j) * D
+                nc.tensor.matmul(gain_all[:, c : c + D], lhsT=ones[:], rhs=gain_rows[:, c : c + D], start=True, stop=True)
+                g[s, j] = keep.tile([P, 2, D], F32, name="g%d%d" % (s, j))
+                nc.vector.tensor_tensor(
+                    out=g[s, j][:].rearrange("p b (i a) -> p b i a", a=2),
+                    in0=rot[:, s, :].rearrange("p (i a b) -> p b i a", a=2, b=2),
+                    in1=gain_all[:, c : c + D]
+                    .rearrange("p (i b) -> p b i", b=2)
+                    .unsqueeze(3)
+                    .to_broadcast([P, 2, D // 2, 2]),
+                    op=ALU.mult,
+                )
+
+        y = {}
+        for s in range(STREAMS):
+            for j in range(3):
+                y[s, j] = psum.tile([P, HD], F32, name="y%d%d" % (s, j))
+                nc.tensor.matmul_mx(
+                    out=y[s, j][:],
+                    lhsT=x_codes[s][:].bitcast(FP8X4),
+                    lhsT_scale=x_scales[s][:],
+                    rhs=w_words[s][:, 2 * HD * j : 2 * HD * (j + 1)].bitcast(FP4X4),
+                    rhs_scale=w_scales[s][:, HD * j : HD * (j + 1)],
+                    start=True,
+                    stop=True,
+                )
+
+        for s in range(STREAMS):
+            for j in range(2):
+                bank = y[s, j]
+                squares = keep.tile([P, HD], F32, name="squares%d%d" % (s, j))
+                sumsq = keep.tile([P, H], F32, name="sumsq%d%d" % (s, j))
+                for h in range(H):
+                    head = slice(h * D, (h + 1) * D)
+                    nc.scalar.activation(
+                        out=squares[:, head], in_=bank[:, head], func=ACT.Square, accum_out=sumsq[:, h : h + 1]
+                    )
+                rstd = keep.tile([P, H], F32, name="rstd%d%d" % (s, j))
+                nc.scalar.activation(out=rstd[:], in_=sumsq[:], func=ACT.Abs_reciprocal_sqrt, bias=eps[:], scale=1.0 / D)
+                term = [keep.tile([P, HD], F32, name="term%d%d%d" % (s, j, b)) for b in range(2)]
+                pairs = bank[:].rearrange("p (h i b) -> p h i b", h=H, b=2)
+                for h in range(H):
+                    head = slice(h * D, (h + 1) * D)
+                    for b in range(2):
+                        nc.vector.scalar_tensor_tensor(
+                            out=term[b][:, head].rearrange("p (i a) -> p i a", a=2),
+                            in0=pairs[:, h, :, b : b + 1].to_broadcast([P, D // 2, 2]),
+                            scalar=rstd[:, h : h + 1],
+                            in1=g[s, j][:, b, :].rearrange("p (i a) -> p i a", a=2),
+                            op0=ALU.mult,
+                            op1=ALU.mult,
+                        )
+                rotated = keep.tile([P, HD], F32, name="rotated%d%d" % (s, j))
+                nc.vector.tensor_tensor(out=rotated[:], in0=term[0][:], in1=term[1][:], op=ALU.add)
+                nc.sync.dma_start(out=outs[j][0, s * P : (s + 1) * P, :], in_=rotated[:])
+
+        for s in range(STREAMS):
+            v_sb = keep.tile([P, HD], F32, name="v_sb%d" % s)
+            nc.scalar.copy(out=v_sb[:], in_=y[s, 2][:])
+            nc.sync.dma_start(out=outs[2][0, s * P : (s + 1) * P, :], in_=v_sb[:])

@@ -21,6 +21,8 @@ HD = H * D
 EPS = 1e-6
 STREAMS = 2
 
+FOLD_AHEAD = 2
+
 FLOPS = 2 * STREAMS * P * DM * 3 * HD
 
 
@@ -48,40 +50,43 @@ def tile_fluxattention_pa_s_kernel(
     gains_dram = ((eqn_scale, ekn_scale), (qn_scale, kn_scale))
     outs = (out_0, out_1, out_2)
 
+    units = [(s, j) for s in range(STREAMS) for j in range(2)]
+
     with ExitStack() as ctx:
         keep = ctx.enter_context(tc.tile_pool(name="keep", bufs=1))
         psum = ctx.enter_context(tc.psum_pool(name="psum", bufs=1))
+        ctx.enter_context(tc.manual_schedule())
 
-        gain_rows = keep.tile([P, 4 * D], BF16, name="gain_rows")
-        nc.vector.memset(gain_rows[:], 0.0)
         w_scales = [keep.tile([P, 3 * HD], U8, name="w_scales%d" % s, align_bytes=64) for s in range(STREAMS)]
-        for s in range(STREAMS):
-            nc.vector.memset(w_scales[s][:].bitcast(I32), 0)
-        ones = keep.tile([P, P], BF16, name="ones")
-        nc.vector.memset(ones[:], 1.0)
+        nc.vector.memset(w_scales[0][:].bitcast(I32), 0)
         eps = keep.tile([P, 1], F32, name="eps")
         nc.vector.memset(eps[:], EPS)
+        gain_rows = keep.tile([P, 4 * D], BF16, name="gain_rows")
+        nc.vector.memset(gain_rows[:], 0.0)
+        ones = keep.tile([P, P], BF16, name="ones")
+        nc.vector.memset(ones[:], 1.0)
+        nc.vector.memset(w_scales[1][:].bitcast(I32), 0)
         identity = keep.tile([P, P], F32, name="identity")
         make_identity(nc, identity[:])
-        warm = keep.tile([P, 1], F32, name="warm")
-        nc.scalar.activation(out=warm[:], in_=eps[:], func=ACT.Abs_reciprocal_sqrt)
 
         x_sb = [keep.tile([P, DM], BF16, name="x_sb%d" % s) for s in range(STREAMS)]
         w_words = [keep.tile([P, 2 * 3 * HD], U8, name="w_words%d" % s, align_bytes=64) for s in range(STREAMS)]
         for s in range(STREAMS):
             nc.sync.dma_start(out=x_sb[s][:], in_=x_dram[s][0])
+        rot = keep.tile([P, STREAMS, 2 * D], BF16, name="rot")
+        nc.scalar.dma_start(out=rot[:], in_=image_rotary_emb.rearrange("(s p) i c -> p s (i c)", s=STREAMS))
         for s in range(STREAMS):
             for r in range(4):
                 nc.sync.dma_start(
                     out=w_scales[s][r:P:32, :].bitcast(I32), in_=scales_dram[s][0, r:16:4, :].bitcast(I32)
                 )
             nc.sync.dma_start(out=w_words[s][:].bitcast(I32), in_=words_dram[s][0].bitcast(I32))
-        rot = keep.tile([P, STREAMS, 2 * D], BF16, name="rot")
-        nc.scalar.dma_start(out=rot[:], in_=image_rotary_emb.rearrange("(s p) i c -> p s (i c)", s=STREAMS))
-        for s in range(STREAMS):
-            for j in range(2):
-                c = (2 * s + j) * D
-                nc.gpsimd.dma_start(out=gain_rows[0:1, c : c + D], in_=gains_dram[s][j].unsqueeze(0))
+        gain_queue = (nc.gpsimd, nc.sync)
+        for n, (s, j) in enumerate(units):
+            gain_queue[s].dma_start(out=gain_rows[0:1, n * D : (n + 1) * D], in_=gains_dram[s][j].unsqueeze(0))
+
+        warm = keep.tile([P, 1], F32, name="warm")
+        nc.scalar.activation(out=warm[:], in_=eps[:], func=ACT.Abs_reciprocal_sqrt)
 
         xt = psum.tile([P, STREAMS, 2, P], F32, name="xt")
         x_codes = []
@@ -100,67 +105,90 @@ def tile_fluxattention_pa_s_kernel(
             x_codes.append(codes)
             x_scales.append(scales)
 
+        y = {}
+
+        def project(s, j):
+            y[s, j] = psum.tile([P, HD], F32, name="y%d%d" % (s, j))
+            nc.tensor.matmul_mx(
+                out=y[s, j][:],
+                lhsT=x_codes[s][:].bitcast(FP8X4),
+                lhsT_scale=x_scales[s][:],
+                rhs=w_words[s][:, 2 * HD * j : 2 * HD * (j + 1)].bitcast(FP4X4),
+                rhs_scale=w_scales[s][:, HD * j : HD * (j + 1)],
+                start=True,
+                stop=True,
+            )
+
         gain_all = psum.tile([P, 4 * D], F32, name="gain_all")
         g = {}
-        for s in range(STREAMS):
-            for j in range(2):
-                c = (2 * s + j) * D
-                nc.tensor.matmul(gain_all[:, c : c + D], lhsT=ones[:], rhs=gain_rows[:, c : c + D], start=True, stop=True)
-                g[s, j] = keep.tile([P, 2, D], F32, name="g%d%d" % (s, j))
-                nc.vector.tensor_tensor(
-                    out=g[s, j][:].rearrange("p b (i a) -> p b i a", a=2),
-                    in0=rot[:, s, :].rearrange("p (i a b) -> p b i a", a=2, b=2),
-                    in1=gain_all[:, c : c + D]
-                    .rearrange("p (i b) -> p b i", b=2)
-                    .unsqueeze(3)
-                    .to_broadcast([P, 2, D // 2, 2]),
-                    op=ALU.mult,
-                )
 
-        y = {}
-        for s in range(STREAMS):
-            for j in range(3):
-                y[s, j] = psum.tile([P, HD], F32, name="y%d%d" % (s, j))
-                nc.tensor.matmul_mx(
-                    out=y[s, j][:],
-                    lhsT=x_codes[s][:].bitcast(FP8X4),
-                    lhsT_scale=x_scales[s][:],
-                    rhs=w_words[s][:, 2 * HD * j : 2 * HD * (j + 1)].bitcast(FP4X4),
-                    rhs_scale=w_scales[s][:, HD * j : HD * (j + 1)],
-                    start=True,
-                    stop=True,
-                )
+        def fold_gain(n):
+            s = units[n][0]
+            cols = slice(n * D, (n + 1) * D)
+            nc.tensor.matmul(gain_all[:, cols], lhsT=ones[:], rhs=gain_rows[:, cols], start=True, stop=True)
+            g[n] = keep.tile([P, 2, D], F32, name="g%d" % n)
+            nc.vector.tensor_tensor(
+                out=g[n][:].rearrange("p b (i a) -> p b i a", a=2),
+                in0=rot[:, s, :].rearrange("p (i a b) -> p b i a", a=2, b=2),
+                in1=gain_all[:, cols].rearrange("p (i b) -> p b i", b=2).unsqueeze(3).to_broadcast([P, 2, D // 2, 2]),
+                op=ALU.mult,
+            )
 
-        for s in range(STREAMS):
-            for j in range(2):
-                bank = y[s, j]
-                squares = keep.tile([P, HD], F32, name="squares%d%d" % (s, j))
-                sumsq = keep.tile([P, H], F32, name="sumsq%d%d" % (s, j))
-                for h in range(H):
-                    head = slice(h * D, (h + 1) * D)
-                    nc.scalar.activation(
-                        out=squares[:, head], in_=bank[:, head], func=ACT.Square, accum_out=sumsq[:, h : h + 1]
+        rstd = {}
+
+        def head_norms(n):
+            bank = y[units[n]]
+            squares = keep.tile([P, HD], F32, name="squares%d" % n)
+            sumsq = keep.tile([P, H], F32, name="sumsq%d" % n)
+            for h in range(H):
+                head = slice(h * D, (h + 1) * D)
+                nc.scalar.activation(
+                    out=squares[:, head], in_=bank[:, head], func=ACT.Square, accum_out=sumsq[:, h : h + 1]
+                )
+            rstd[n] = keep.tile([P, H], F32, name="rstd%d" % n)
+            nc.scalar.activation(out=rstd[n][:], in_=sumsq[:], func=ACT.Abs_reciprocal_sqrt, bias=eps[:], scale=1.0 / D)
+
+        term = {}
+
+        def products(n):
+            term[n] = [keep.tile([P, HD], F32, name="term%d%d" % (n, b)) for b in range(2)]
+            pairs = y[units[n]][:].rearrange("p (h i b) -> p h i b", h=H, b=2)
+            for h in range(H):
+                head = slice(h * D, (h + 1) * D)
+                for b in range(2):
+                    nc.vector.scalar_tensor_tensor(
+                        out=term[n][b][:, head].rearrange("p (i a) -> p i a", a=2),
+                        in0=pairs[:, h, :, b : b + 1].to_broadcast([P, D // 2, 2]),
+                        scalar=rstd[n][:, h : h + 1],
+                        in1=g[n][:, b, :].rearrange("p (i a) -> p i a", a=2),
+                        op0=ALU.mult,
+                        op1=ALU.mult,
                     )
-                rstd = keep.tile([P, H], F32, name="rstd%d%d" % (s, j))
-                nc.scalar.activation(out=rstd[:], in_=sumsq[:], func=ACT.Abs_reciprocal_sqrt, bias=eps[:], scale=1.0 / D)
-                term = [keep.tile([P, HD], F32, name="term%d%d%d" % (s, j, b)) for b in range(2)]
-                pairs = bank[:].rearrange("p (h i b) -> p h i b", h=H, b=2)
-                for h in range(H):
-                    head = slice(h * D, (h + 1) * D)
-                    for b in range(2):
-                        nc.vector.scalar_tensor_tensor(
-                            out=term[b][:, head].rearrange("p (i a) -> p i a", a=2),
-                            in0=pairs[:, h, :, b : b + 1].to_broadcast([P, D // 2, 2]),
-                            scalar=rstd[:, h : h + 1],
-                            in1=g[s, j][:, b, :].rearrange("p (i a) -> p i a", a=2),
-                            op0=ALU.mult,
-                            op1=ALU.mult,
-                        )
-                rotated = keep.tile([P, HD], F32, name="rotated%d%d" % (s, j))
-                nc.vector.tensor_tensor(out=rotated[:], in0=term[0][:], in1=term[1][:], op=ALU.add)
-                nc.sync.dma_start(out=outs[j][0, s * P : (s + 1) * P, :], in_=rotated[:])
 
+        def add_and_store(n):
+            s, j = units[n]
+            rotated = keep.tile([P, HD], F32, name="rotated%d" % n)
+            nc.vector.tensor_tensor(out=rotated[:], in0=term[n][0][:], in1=term[n][1][:], op=ALU.add)
+            nc.sync.dma_start(out=outs[j][0, s * P : (s + 1) * P, :], in_=rotated[:])
+
+        for j in range(2):
+            project(0, j)
+        for n in range(FOLD_AHEAD):
+            fold_gain(n)
+        for j in range(2):
+            project(1, j)
+        for s in range(STREAMS):
+            project(s, 2)
+
+        for n in range(len(units)):
+            head_norms(n)
         for s in range(STREAMS):
             v_sb = keep.tile([P, HD], F32, name="v_sb%d" % s)
             nc.scalar.copy(out=v_sb[:], in_=y[s, 2][:])
-            nc.sync.dma_start(out=outs[2][0, s * P : (s + 1) * P, :], in_=v_sb[:])
+            nc.scalar.dma_start(out=outs[2][0, s * P : (s + 1) * P, :], in_=v_sb[:])
+
+        for n in range(len(units)):
+            products(n)
+            if n + FOLD_AHEAD < len(units):
+                fold_gain(n + FOLD_AHEAD)
+            add_and_store(n)

@@ -168,7 +168,8 @@ def tile_fluxattention_pa_s_kernel(
         def add_and_store(n):
             s, j = units[n]
             rotated = keep.tile([P, HD], F32, name="rotated%d" % n)
-            nc.vector.tensor_tensor(out=rotated[:], in0=term[n][0][:], in1=term[n][1][:], op=ALU.add)
+            adder = nc.gpsimd if n + 1 < len(units) else nc.vector
+            adder.tensor_tensor(out=rotated[:], in0=term[n][0][:], in1=term[n][1][:], op=ALU.add)
             nc.sync.dma_start(out=outs[j][0, s * P : (s + 1) * P, :], in_=rotated[:])
 
         for j in range(2):

@@ -21,7 +21,9 @@ HD = H * D
 EPS = 1e-6
 STREAMS = 2
 
-FOLD_AHEAD = 2
+HALF = HD // 2
+HH = H // 2
+VECTOR_ADDS_FROM = 6
 
 FLOPS = 2 * STREAMS * P * DM * 3 * HD
 
@@ -51,53 +53,68 @@ def tile_fluxattention_pa_s_kernel(
     outs = (out_0, out_1, out_2)
 
     units = [(s, j) for s in range(STREAMS) for j in range(2)]
+    halves = [(s, j, e) for s, j in units for e in range(2)]
 
     with ExitStack() as ctx:
         keep = ctx.enter_context(tc.tile_pool(name="keep", bufs=1))
         psum = ctx.enter_context(tc.psum_pool(name="psum", bufs=1))
         ctx.enter_context(tc.manual_schedule())
 
+        gain_rows = keep.tile([P, 4 * D], BF16, name="gain_rows")
+        nc.gpsimd.memset(gain_rows[:], 0.0)
         w_scales = [keep.tile([P, 3 * HD], U8, name="w_scales%d" % s, align_bytes=64) for s in range(STREAMS)]
         nc.vector.memset(w_scales[0][:].bitcast(I32), 0)
         eps = keep.tile([P, 1], F32, name="eps")
         nc.vector.memset(eps[:], EPS)
-        gain_rows = keep.tile([P, 4 * D], BF16, name="gain_rows")
-        nc.vector.memset(gain_rows[:], 0.0)
         ones = keep.tile([P, P], BF16, name="ones")
         nc.vector.memset(ones[:], 1.0)
         nc.vector.memset(w_scales[1][:].bitcast(I32), 0)
-        identity = keep.tile([P, P], F32, name="identity")
-        make_identity(nc, identity[:])
 
         x_sb = [keep.tile([P, DM], BF16, name="x_sb%d" % s) for s in range(STREAMS)]
         w_words = [keep.tile([P, 2 * 3 * HD], U8, name="w_words%d" % s, align_bytes=64) for s in range(STREAMS)]
+        rot = keep.tile([P, STREAMS, 2 * D], BF16, name="rot")
+
+        def load_scales(s, r):
+            nc.sync.dma_start(out=w_scales[s][r:P:32, :].bitcast(I32), in_=scales_dram[s][0, r:16:4, :].bitcast(I32))
+
+        def load_gain(queue, n):
+            s, j = units[n]
+            queue.dma_start(out=gain_rows[0:1, n * D : (n + 1) * D], in_=gains_dram[s][j].unsqueeze(0))
+
         for s in range(STREAMS):
             nc.sync.dma_start(out=x_sb[s][:], in_=x_dram[s][0])
-        rot = keep.tile([P, STREAMS, 2 * D], BF16, name="rot")
         nc.scalar.dma_start(out=rot[:], in_=image_rotary_emb.rearrange("(s p) i c -> p s (i c)", s=STREAMS))
-        for s in range(STREAMS):
-            for r in range(4):
-                nc.sync.dma_start(
-                    out=w_scales[s][r:P:32, :].bitcast(I32), in_=scales_dram[s][0, r:16:4, :].bitcast(I32)
-                )
-            nc.sync.dma_start(out=w_words[s][:].bitcast(I32), in_=words_dram[s][0].bitcast(I32))
-        gain_queue = (nc.gpsimd, nc.sync)
-        for n, (s, j) in enumerate(units):
-            gain_queue[s].dma_start(out=gain_rows[0:1, n * D : (n + 1) * D], in_=gains_dram[s][j].unsqueeze(0))
+        for r in range(4):
+            load_scales(0, r)
+        nc.sync.dma_start(out=w_words[0][:].bitcast(I32), in_=words_dram[0][0].bitcast(I32))
+        for n in range(1, len(units)):
+            load_gain(nc.sync, n)
+        nc.sync.dma_start(out=w_words[1][:].bitcast(I32), in_=words_dram[1][0].bitcast(I32))
+        for r in range(4):
+            load_scales(1, r)
+        identity = keep.tile([P, P], F32, name="identity")
+        make_identity(nc, identity[:])
+        load_gain(nc.gpsimd, 0)
 
         warm = keep.tile([P, 1], F32, name="warm")
         nc.scalar.activation(out=warm[:], in_=eps[:], func=ACT.Abs_reciprocal_sqrt)
 
-        xt = psum.tile([P, STREAMS, 2, P], F32, name="xt")
+        xt0 = psum.tile([P, 2 * P], F32, name="xt0")
+        shared = psum.tile([P, 4 * D + 2 * P], F32, name="shared")
+        gain_all = shared[:, 0 : 4 * D]
+        xt = [xt0[:].rearrange("p (u r) -> p u r", u=2), shared[:, 4 * D : 4 * D + 2 * P].rearrange("p (u r) -> p u r", u=2)]
         x_codes = []
         x_scales = []
-        for s in range(STREAMS):
+
+        def transposes(s):
             for u in range(2):
-                nc.tensor.transpose(xt[:, s, u, :], x_sb[s][:].bitcast(F32)[:, u : DM // 2 : 2], identity[:])
+                nc.tensor.transpose(xt[s][:, u, :], x_sb[s][:].bitcast(F32)[:, u : DM // 2 : 2], identity[:])
+
+        def quantise(s):
             grouped = keep.tile([P, 4 * P], BF16, name="grouped%d" % s, align_bytes=64)
-            nc.vector.tensor_copy(
+            nc.scalar.copy(
                 out=grouped[:].bitcast(F32).rearrange("p (r u) -> p r u", u=2),
-                in_=xt[:, s].rearrange("p u r -> p r u"),
+                in_=xt[s].rearrange("p u r -> p r u"),
             )
             codes = keep.tile([P, P], U32, name="x_codes%d" % s, align_bytes=64)
             scales = keep.tile([P, P], U8, name="x_scales%d" % s, align_bytes=64)
@@ -105,91 +122,118 @@ def tile_fluxattention_pa_s_kernel(
             x_codes.append(codes)
             x_scales.append(scales)
 
-        y = {}
-
-        def project(s, j):
-            y[s, j] = psum.tile([P, HD], F32, name="y%d%d" % (s, j))
+        def multiply(out, s, col, width):
             nc.tensor.matmul_mx(
-                out=y[s, j][:],
+                out=out,
                 lhsT=x_codes[s][:].bitcast(FP8X4),
                 lhsT_scale=x_scales[s][:],
-                rhs=w_words[s][:, 2 * HD * j : 2 * HD * (j + 1)].bitcast(FP4X4),
-                rhs_scale=w_scales[s][:, HD * j : HD * (j + 1)],
+                rhs=w_words[s][:, 2 * col : 2 * (col + width)].bitcast(FP4X4),
+                rhs_scale=w_scales[s][:, col : col + width],
                 start=True,
                 stop=True,
             )
 
-        gain_all = psum.tile([P, 4 * D], F32, name="gain_all")
+        qk = [psum.tile([P, HD], F32, name="qk%d" % b) for b in range(4)]
+        v_bank = [psum.tile([P, HD], F32, name="v_bank%d" % s) for s in range(STREAMS)]
+
+        def piece(m):
+            s, j, e = halves[m]
+            return qk[2 * j + e][:, s * HALF : (s + 1) * HALF]
+
+        def project(m):
+            s, j, e = halves[m]
+            multiply(piece(m), s, j * HD + e * HALF, HALF)
+
         g = {}
 
         def fold_gain(n):
             s = units[n][0]
             cols = slice(n * D, (n + 1) * D)
-            nc.tensor.matmul(gain_all[:, cols], lhsT=ones[:], rhs=gain_rows[:, cols], start=True, stop=True)
-            g[n] = keep.tile([P, 2, D], F32, name="g%d" % n)
+            g[n] = keep.tile([P, 2 * D], F32, name="g%d" % n)
             nc.vector.tensor_tensor(
-                out=g[n][:].rearrange("p b (i a) -> p b i a", a=2),
-                in0=rot[:, s, :].rearrange("p (i a b) -> p b i a", a=2, b=2),
-                in1=gain_all[:, cols].rearrange("p (i b) -> p b i", b=2).unsqueeze(3).to_broadcast([P, 2, D // 2, 2]),
+                out=g[n][:].rearrange("p (i b a) -> p i b a", a=2, b=2),
+                in0=rot[:, s, :].rearrange("p (i a b) -> p i b a", a=2, b=2),
+                in1=gain_all[:, cols].rearrange("p (i b) -> p i b", b=2).unsqueeze(3).to_broadcast([P, D // 2, 2, 2]),
                 op=ALU.mult,
             )
 
         rstd = {}
 
-        def head_norms(n):
-            bank = y[units[n]]
-            squares = keep.tile([P, HD], F32, name="squares%d" % n)
-            sumsq = keep.tile([P, H], F32, name="sumsq%d" % n)
-            for h in range(H):
+        def norms(m):
+            squares = keep.tile([P, HALF], F32, name="squares%d" % m)
+            sumsq = keep.tile([P, HH], F32, name="sumsq%d" % m)
+            for h in range(HH):
                 head = slice(h * D, (h + 1) * D)
                 nc.scalar.activation(
-                    out=squares[:, head], in_=bank[:, head], func=ACT.Square, accum_out=sumsq[:, h : h + 1]
+                    out=squares[:, head], in_=piece(m)[:, head], func=ACT.Square, accum_out=sumsq[:, h : h + 1]
                 )
-            rstd[n] = keep.tile([P, H], F32, name="rstd%d" % n)
-            nc.scalar.activation(out=rstd[n][:], in_=sumsq[:], func=ACT.Abs_reciprocal_sqrt, bias=eps[:], scale=1.0 / D)
+            rstd[m] = keep.tile([P, HH], F32, name="rstd%d" % m)
+            nc.scalar.activation(out=rstd[m][:], in_=sumsq[:], func=ACT.Abs_reciprocal_sqrt, bias=eps[:], scale=1.0 / D)
 
         term = {}
 
-        def products(n):
-            term[n] = [keep.tile([P, HD], F32, name="term%d%d" % (n, b)) for b in range(2)]
-            pairs = y[units[n]][:].rearrange("p (h i b) -> p h i b", h=H, b=2)
-            for h in range(H):
-                head = slice(h * D, (h + 1) * D)
-                for b in range(2):
-                    nc.vector.scalar_tensor_tensor(
-                        out=term[n][b][:, head].rearrange("p (i a) -> p i a", a=2),
-                        in0=pairs[:, h, :, b : b + 1].to_broadcast([P, D // 2, 2]),
-                        scalar=rstd[n][:, h : h + 1],
-                        in1=g[n][:, b, :].rearrange("p (i a) -> p i a", a=2),
-                        op0=ALU.mult,
-                        op1=ALU.mult,
-                    )
+        def products(m):
+            term[m] = keep.tile([P, 2 * HALF], F32, name="term%d" % m)
+            for h in range(HH):
+                nc.vector.scalar_tensor_tensor(
+                    out=term[m][:, 2 * h * D : 2 * (h + 1) * D].rearrange("p (c a) -> p c a", a=2),
+                    in0=piece(m)[:, h * D : (h + 1) * D].unsqueeze(2).to_broadcast([P, D, 2]),
+                    scalar=rstd[m][:, h : h + 1],
+                    in1=g[m // 2][:].rearrange("p (c a) -> p c a", a=2),
+                    op0=ALU.mult,
+                    op1=ALU.mult,
+                )
 
-        def add_and_store(n):
-            s, j = units[n]
-            rotated = keep.tile([P, HD], F32, name="rotated%d" % n)
-            adder = nc.gpsimd if n + 1 < len(units) else nc.vector
-            adder.tensor_tensor(out=rotated[:], in0=term[n][0][:], in1=term[n][1][:], op=ALU.add)
-            nc.sync.dma_start(out=outs[j][0, s * P : (s + 1) * P, :], in_=rotated[:])
+        def add_and_store(m):
+            s, j, e = halves[m]
+            rotated = keep.tile([P, HALF], F32, name="rotated%d" % m)
+            both = term[m][:].rearrange("p (c b a) -> p c b a", b=2, a=2)
+            adder = nc.gpsimd if m < VECTOR_ADDS_FROM else nc.vector
+            adder.tensor_tensor(
+                out=rotated[:].rearrange("p (c a) -> p c a", a=2), in0=both[:, :, 0, :], in1=both[:, :, 1, :], op=ALU.add
+            )
+            nc.sync.dma_start(out=outs[j][0, s * P : (s + 1) * P, e * HALF : (e + 1) * HALF], in_=rotated[:])
 
-        for j in range(2):
-            project(0, j)
-        for n in range(FOLD_AHEAD):
-            fold_gain(n)
-        for j in range(2):
-            project(1, j)
-        for s in range(STREAMS):
-            project(s, 2)
-
-        for n in range(len(units)):
-            head_norms(n)
-        for s in range(STREAMS):
+        def pass_v(s):
             v_sb = keep.tile([P, HD], F32, name="v_sb%d" % s)
-            nc.scalar.copy(out=v_sb[:], in_=y[s, 2][:])
-            nc.scalar.dma_start(out=outs[2][0, s * P : (s + 1) * P, :], in_=v_sb[:])
+            nc.scalar.copy(out=v_sb[:], in_=v_bank[s][:])
+            nc.sync.dma_start(out=outs[2][0, s * P : (s + 1) * P, :], in_=v_sb[:])
 
-        for n in range(len(units)):
-            products(n)
-            if n + FOLD_AHEAD < len(units):
-                fold_gain(n + FOLD_AHEAD)
-            add_and_store(n)
+        def spread_gains(first, last):
+            cols = slice(first * D, last * D)
+            nc.tensor.matmul(gain_all[:, cols], lhsT=ones[:], rhs=gain_rows[:, cols], start=True, stop=True)
+
+        transposes(0)
+        quantise(0)
+        transposes(1)
+        quantise(1)
+        for m in range(2):
+            project(m)
+        spread_gains(0, 1)
+        fold_gain(0)
+        for m in range(2, 4):
+            project(m)
+        multiply(v_bank[0][:], 0, 2 * HD, HD)
+        spread_gains(1, 4)
+        count = len(halves)
+        for step in range(count + 2):
+            if step < count:
+                norms(step)
+            if step == 1:
+                pass_v(0)
+            if 1 <= step <= count:
+                m = step - 1
+                products(m)
+                if m == 1:
+                    for n in range(1, len(units)):
+                        fold_gain(n)
+                if m + 4 < count:
+                    project(m + 4)
+                if m == 3:
+                    multiply(v_bank[1][:], 1, 2 * HD, HD)
+            if step == count - 1:
+                pass_v(1)
+            if step >= 2 and step - 2 < VECTOR_ADDS_FROM:
+                add_and_store(step - 2)
+        for m in range(VECTOR_ADDS_FROM, count):
+            add_and_store(m)

@@ -24,6 +24,7 @@ STREAMS = 2
 HALF = HD // 2
 HH = H // 2
 VECTOR_ADDS_FROM = 6
+WARM_UPS = 4
 
 FLOPS = 2 * STREAMS * P * DM * 3 * HD
 
@@ -60,6 +61,8 @@ def tile_fluxattention_pa_s_kernel(
         psum = ctx.enter_context(tc.psum_pool(name="psum", bufs=1))
         ctx.enter_context(tc.manual_schedule())
 
+        idle = keep.tile([P, P], F32, name="idle")
+        nc.gpsimd.memset(idle[:], 0.0)
         gain_rows = keep.tile([P, 4 * D], BF16, name="gain_rows")
         nc.gpsimd.memset(gain_rows[:], 0.0)
         w_scales = [keep.tile([P, 3 * HD], U8, name="w_scales%d" % s, align_bytes=64) for s in range(STREAMS)]
@@ -203,6 +206,8 @@ def tile_fluxattention_pa_s_kernel(
             cols = slice(first * D, last * D)
             nc.tensor.matmul(gain_all[:, cols], lhsT=ones[:], rhs=gain_rows[:, cols], start=True, stop=True)
 
+        for w in range(WARM_UPS):
+            nc.tensor.matmul(xt0[:, 0:P], lhsT=idle[:], rhs=idle[:], start=True, stop=True)
         transposes(0)
         quantise(0)
         transposes(1)

@@ -90,14 +90,13 @@ def tile_fluxattention_pa_s_kernel(
         for r in range(4):
             load_scales(0, r)
         nc.sync.dma_start(out=w_words[0][:].bitcast(I32), in_=words_dram[0][0].bitcast(I32))
-        for n in range(1, len(units)):
+        for n in range(len(units)):
             load_gain(nc.sync, n)
         nc.sync.dma_start(out=w_words[1][:].bitcast(I32), in_=words_dram[1][0].bitcast(I32))
         for r in range(4):
             load_scales(1, r)
         identity = keep.tile([P, P], F32, name="identity")
         make_identity(nc, identity[:])
-        load_gain(nc.gpsimd, 0)
 
         warm = keep.tile([P, 1], F32, name="warm")
         nc.scalar.activation(out=warm[:], in_=eps[:], func=ACT.Abs_reciprocal_sqrt)

@@ -23,7 +23,7 @@ STREAMS = 2
 
 HALF = HD // 2
 HH = H // 2
-VECTOR_ADDS_FROM = 6
+VECTOR_ADDS_FROM = 7
 WARM_UPS = 4
 
 FLOPS = 2 * STREAMS * P * DM * 3 * HD

@@ -24,7 +24,6 @@ STREAMS = 2
 HALF = HD // 2
 HH = H // 2
 VECTOR_ADDS_FROM = 7
-WARM_UPS = 4
 
 FLOPS = 2 * STREAMS * P * DM * 3 * HD
 
@@ -61,8 +60,6 @@ def tile_fluxattention_pa_s_kernel(
         psum = ctx.enter_context(tc.psum_pool(name="psum", bufs=1))
         ctx.enter_context(tc.manual_schedule())
 
-        idle = keep.tile([P, P], F32, name="idle")
-        nc.gpsimd.memset(idle[:], 0.0)
         gain_rows = keep.tile([P, 4 * D], BF16, name="gain_rows")
         nc.gpsimd.memset(gain_rows[:], 0.0)
         w_scales = [keep.tile([P, 3 * HD], U8, name="w_scales%d" % s, align_bytes=64) for s in range(STREAMS)]
@@ -205,8 +202,6 @@ def tile_fluxattention_pa_s_kernel(
             cols = slice(first * D, last * D)
             nc.tensor.matmul(gain_all[:, cols], lhsT=ones[:], rhs=gain_rows[:, cols], start=True, stop=True)
 
-        for w in range(WARM_UPS):
-            nc.tensor.matmul(xt0[:, 0:P], lhsT=idle[:], rhs=idle[:], start=True, stop=True)
         transposes(0)
         quantise(0)
         transposes(1)

@@ -158,16 +158,23 @@ def tile_fluxattention_pa_s_kernel(
 
         rstd = {}
 
-        def norms(m):
-            squares = keep.tile([P, HALF], F32, name="squares%d" % m)
-            sumsq = keep.tile([P, HH], F32, name="sumsq%d" % m)
-            for h in range(HH):
-                head = slice(h * D, (h + 1) * D)
-                nc.scalar.activation(
-                    out=squares[:, head], in_=piece(m)[:, head], func=ACT.Square, accum_out=sumsq[:, h : h + 1]
-                )
+        squares = {}
+        sumsq = {}
+
+        def square(m, h):
+            if h == 0:
+                squares[m] = keep.tile([P, HALF], F32, name="squares%d" % m)
+                sumsq[m] = keep.tile([P, HH], F32, name="sumsq%d" % m)
+            head = slice(h * D, (h + 1) * D)
+            nc.scalar.activation(
+                out=squares[m][:, head], in_=piece(m)[:, head], func=ACT.Square, accum_out=sumsq[m][:, h : h + 1]
+            )
+
+        def invert(m):
             rstd[m] = keep.tile([P, HH], F32, name="rstd%d" % m)
-            nc.scalar.activation(out=rstd[m][:], in_=sumsq[:], func=ACT.Abs_reciprocal_sqrt, bias=eps[:], scale=1.0 / D)
+            nc.scalar.activation(
+                out=rstd[m][:], in_=sumsq[m][:], func=ACT.Abs_reciprocal_sqrt, bias=eps[:], scale=1.0 / D
+            )
 
         term = {}
 
@@ -193,10 +200,15 @@ def tile_fluxattention_pa_s_kernel(
             )
             nc.sync.dma_start(out=outs[j][0, s * P : (s + 1) * P, e * HALF : (e + 1) * HALF], in_=rotated[:])
 
-        def pass_v(s):
-            v_sb = keep.tile([P, HD], F32, name="v_sb%d" % s)
-            nc.scalar.copy(out=v_sb[:], in_=v_bank[s][:])
-            nc.sync.dma_start(out=outs[2][0, s * P : (s + 1) * P, :], in_=v_sb[:])
+        v_sb = {}
+
+        def copy_v(s, e):
+            if e == 0:
+                v_sb[s] = keep.tile([P, HD], F32, name="v_sb%d" % s)
+            cols = slice(e * HALF, (e + 1) * HALF)
+            nc.scalar.copy(out=v_sb[s][:, cols], in_=v_bank[s][:, cols])
+            if e == 1:
+                nc.sync.dma_start(out=outs[2][0, s * P : (s + 1) * P, :], in_=v_sb[s][:])
 
         def spread_gains(first, last):
             cols = slice(first * D, last * D)
@@ -215,11 +227,21 @@ def tile_fluxattention_pa_s_kernel(
         multiply(v_bank[0][:], 0, 2 * HD, HD)
         spread_gains(1, 4)
         count = len(halves)
+        copies = {1: (0, 0), 2: (0, 1), count - 2: (1, 0), count - 1: (1, 1)}
+        ahead = 2
+        squared = 0
         for step in range(count + 2):
             if step < count:
-                norms(step)
-            if step == 1:
-                pass_v(0)
+                for h in range(squared, HH):
+                    square(step, h)
+                squared = 0
+                if step in copies:
+                    copy_v(*copies[step])
+                else:
+                    for h in range(ahead):
+                        square(step + 1, h)
+                    squared = ahead
+                invert(step)
             if 1 <= step <= count:
                 m = step - 1
                 products(m)
@@ -230,8 +252,6 @@ def tile_fluxattention_pa_s_kernel(
                     project(m + 4)
                 if m == 3:
                     multiply(v_bank[1][:], 1, 2 * HD, HD)
-            if step == count - 1:
-                pass_v(1)
             if step >= 2 and step - 2 < VECTOR_ADDS_FROM:
                 add_and_store(step - 2)
         for m in range(VECTOR_ADDS_FROM, count):

@@ -227,7 +227,7 @@ def tile_fluxattention_pa_s_kernel(
         multiply(v_bank[0][:], 0, 2 * HD, HD)
         spread_gains(1, 4)
         count = len(halves)
-        copies = {1: (0, 0), 2: (0, 1), count - 2: (1, 0), count - 1: (1, 1)}
+        copies = {1: (0, 0), 2: (0, 1), 4: (1, 0), 5: (1, 1)}
         ahead = 2
         squared = 0
         for step in range(count + 2):
@@ -237,7 +237,7 @@ def tile_fluxattention_pa_s_kernel(
                 squared = 0
                 if step in copies:
                     copy_v(*copies[step])
-                else:
+                elif step + 1 < count:
                     for h in range(ahead):
                         square(step + 1, h)
                     squared = ahead
@@ -250,7 +250,7 @@ def tile_fluxattention_pa_s_kernel(
                         fold_gain(n)
                 if m + 4 < count:
                     project(m + 4)
-                if m == 3:
+                if m == 1:
                     multiply(v_bank[1][:], 1, 2 * HD, HD)
             if step >= 2 and step - 2 < VECTOR_ADDS_FROM:
                 add_and_store(step - 2)

@@ -170,10 +170,15 @@ def tile_fluxattention_pa_s_kernel(
                 out=squares[m][:, head], in_=piece(m)[:, head], func=ACT.Square, accum_out=sumsq[m][:, h : h + 1]
             )
 
-        def invert(m):
-            rstd[m] = keep.tile([P, HH], F32, name="rstd%d" % m)
+        def invert(m, first, last):
+            if first == 0:
+                rstd[m] = keep.tile([P, HH], F32, name="rstd%d" % m)
             nc.scalar.activation(
-                out=rstd[m][:], in_=sumsq[m][:], func=ACT.Abs_reciprocal_sqrt, bias=eps[:], scale=1.0 / D
+                out=rstd[m][:, first:last],
+                in_=sumsq[m][:, first:last],
+                func=ACT.Abs_reciprocal_sqrt,
+                bias=eps[:],
+                scale=1.0 / D,
             )
 
         term = {}
@@ -207,8 +212,11 @@ def tile_fluxattention_pa_s_kernel(
                 v_sb[s] = keep.tile([P, HD], F32, name="v_sb%d" % s)
             cols = slice(e * HALF, (e + 1) * HALF)
             nc.scalar.copy(out=v_sb[s][:, cols], in_=v_bank[s][:, cols])
-            if e == 1:
-                nc.sync.dma_start(out=outs[2][0, s * P : (s + 1) * P, :], in_=v_sb[s][:])
+            first = 0 if s == 0 else e * HALF
+            if s == 1 or e == 1:
+                nc.sync.dma_start(
+                    out=outs[2][0, s * P : (s + 1) * P, first : (e + 1) * HALF], in_=v_sb[s][:, first : (e + 1) * HALF]
+                )
 
         def spread_gains(first, last):
             cols = slice(first * D, last * D)
@@ -227,7 +235,7 @@ def tile_fluxattention_pa_s_kernel(
         multiply(v_bank[0][:], 0, 2 * HD, HD)
         spread_gains(1, 4)
         count = len(halves)
-        copies = {1: (0, 0), 2: (0, 1), 4: (1, 0), 5: (1, 1)}
+        copies = {2: (0, 0), 3: (0, 1), 5: (1, 0)}
         ahead = 2
         squared = 0
         for step in range(count + 2):
@@ -235,13 +243,19 @@ def tile_fluxattention_pa_s_kernel(
                 for h in range(squared, HH):
                     square(step, h)
                 squared = 0
+                inverted = 0
+                if step == 0:
+                    inverted = HH // 2
+                    invert(0, 0, inverted)
                 if step in copies:
                     copy_v(*copies[step])
                 elif step + 1 < count:
                     for h in range(ahead):
                         square(step + 1, h)
                     squared = ahead
-                invert(step)
+                invert(step, inverted, HH)
+                if step == count - 1:
+                    copy_v(1, 1)
             if 1 <= step <= count:
                 m = step - 1
                 products(m)

@@ -23,7 +23,7 @@ STREAMS = 2
 
 HALF = HD // 2
 HH = H // 2
-VECTOR_ADDS_FROM = 7
+VECTOR_ADDS_FROM = 6
 
 FLOPS = 2 * STREAMS * P * DM * 3 * HD
 
@@ -228,12 +228,13 @@ def tile_fluxattention_pa_s_kernel(
         quantise(1)
         for m in range(2):
             project(m)
-        spread_gains(0, 1)
-        fold_gain(0)
+        spread_gains(0, 2)
+        for n in range(2):
+            fold_gain(n)
         for m in range(2, 4):
             project(m)
         multiply(v_bank[0][:], 0, 2 * HD, HD)
-        spread_gains(1, 4)
+        spread_gains(2, 4)
         count = len(halves)
         copies = {2: (0, 0), 3: (0, 1), 5: (1, 0)}
         ahead = 2
@@ -260,7 +261,7 @@ def tile_fluxattention_pa_s_kernel(
                 m = step - 1
                 products(m)
                 if m == 1:
-                    for n in range(1, len(units)):
+                    for n in range(2, len(units)):
                         fold_gain(n)
                 if m + 4 < count:
                     project(m + 4)

@@ -23,6 +23,7 @@ STREAMS = 2
 
 HALF = HD // 2
 HH = H // 2
+TENSOR_ADDS = 3
 VECTOR_ADDS_FROM = 6
 
 FLOPS = 2 * STREAMS * P * DM * 3 * HD
@@ -86,10 +87,18 @@ def tile_fluxattention_pa_s_kernel(
         nc.scalar.dma_start(out=rot[:], in_=image_rotary_emb.rearrange("(s p) i c -> p s (i c)", s=STREAMS))
         for r in range(4):
             load_scales(0, r)
-        nc.sync.dma_start(out=w_words[0][:].bitcast(I32), in_=words_dram[0][0].bitcast(I32))
-        for n in range(len(units)):
+
+        def load_words(s, first, last):
+            cols = slice(2 * first, 2 * last)
+            nc.sync.dma_start(out=w_words[s][:, cols].bitcast(I32), in_=words_dram[s][0, :, cols].bitcast(I32))
+
+        load_words(0, 0, HD)
+        for n in range(2):
             load_gain(nc.sync, n)
-        nc.sync.dma_start(out=w_words[1][:].bitcast(I32), in_=words_dram[1][0].bitcast(I32))
+        load_words(0, HD, 3 * HD)
+        for n in range(2, len(units)):
+            load_gain(nc.sync, n)
+        load_words(1, 0, 3 * HD)
         for r in range(4):
             load_scales(1, r)
         identity = keep.tile([P, P], F32, name="identity")
@@ -195,14 +204,37 @@ def tile_fluxattention_pa_s_kernel(
                     op1=ALU.mult,
                 )
 
-        def add_and_store(m):
-            s, j, e = halves[m]
-            rotated = keep.tile([P, HALF], F32, name="rotated%d" % m)
+        def both_terms(m):
             both = term[m][:].rearrange("p (c b a) -> p c b a", b=2, a=2)
-            adder = nc.gpsimd if m < VECTOR_ADDS_FROM else nc.vector
-            adder.tensor_tensor(
-                out=rotated[:].rearrange("p (c a) -> p c a", a=2), in0=both[:, :, 0, :], in1=both[:, :, 1, :], op=ALU.add
+            return [both[:, :, b, :] for b in range(2)]
+
+        def add_and_store(engine, m):
+            terms = both_terms(m)
+            rotated = keep.tile([P, HALF], F32, name="rotated%d" % m)
+            engine.tensor_tensor(
+                out=rotated[:].rearrange("p (c a) -> p c a", a=2), in0=terms[0], in1=terms[1], op=ALU.add
             )
+            store(m, rotated)
+
+        tensor_sum = v_bank[0][:, 0:HALF]
+
+        def add_on_tensor(m):
+            for b, one_term in enumerate(both_terms(m)):
+                nc.tensor.matmul(
+                    tensor_sum.rearrange("p (c a) -> p c a", a=2),
+                    lhsT=identity[:],
+                    rhs=one_term,
+                    start=b == 0,
+                    stop=b == 1,
+                )
+
+        def copy_and_store(m):
+            rotated = keep.tile([P, HALF], F32, name="rotated%d" % m)
+            nc.scalar.copy(out=rotated[:], in_=tensor_sum)
+            store(m, rotated)
+
+        def store(m, rotated):
+            s, j, e = halves[m]
             nc.sync.dma_start(out=outs[j][0, s * P : (s + 1) * P, e * HALF : (e + 1) * HALF], in_=rotated[:])
 
         v_sb = {}
@@ -236,7 +268,7 @@ def tile_fluxattention_pa_s_kernel(
         multiply(v_bank[0][:], 0, 2 * HD, HD)
         spread_gains(2, 4)
         count = len(halves)
-        copies = {2: (0, 0), 3: (0, 1), 5: (1, 0)}
+        copies = {3: (0, 0), 4: (0, 1), 6: (1, 0)}
         ahead = 2
         squared = 0
         for step in range(count + 2):
@@ -257,6 +289,7 @@ def tile_fluxattention_pa_s_kernel(
                 invert(step, inverted, HH)
                 if step == count - 1:
                     copy_v(1, 1)
+                    copy_and_store(TENSOR_ADDS)
             if 1 <= step <= count:
                 m = step - 1
                 products(m)
@@ -267,7 +300,9 @@ def tile_fluxattention_pa_s_kernel(
                     project(m + 4)
                 if m == 1:
                     multiply(v_bank[1][:], 1, 2 * HD, HD)
-            if step >= 2 and step - 2 < VECTOR_ADDS_FROM:
-                add_and_store(step - 2)
+                if m == TENSOR_ADDS:
+                    add_on_tensor(m)
+            if 2 <= step < VECTOR_ADDS_FROM + 2 and step - 2 != TENSOR_ADDS:
+                add_and_store(nc.gpsimd, step - 2)
         for m in range(VECTOR_ADDS_FROM, count):
-            add_and_store(m)
+            add_and_store(nc.vector, m)

@@ -88,17 +88,13 @@ def tile_fluxattention_pa_s_kernel(
         for r in range(4):
             load_scales(0, r)
 
-        def load_words(s, first, last):
-            cols = slice(2 * first, 2 * last)
-            nc.sync.dma_start(out=w_words[s][:, cols].bitcast(I32), in_=words_dram[s][0, :, cols].bitcast(I32))
+        def load_words(s):
+            nc.sync.dma_start(out=w_words[s][:].bitcast(I32), in_=words_dram[s][0].bitcast(I32))
 
-        load_words(0, 0, HD)
-        for n in range(2):
+        load_words(0)
+        for n in range(len(units)):
             load_gain(nc.sync, n)
-        load_words(0, HD, 3 * HD)
-        for n in range(2, len(units)):
-            load_gain(nc.sync, n)
-        load_words(1, 0, 3 * HD)
+        load_words(1)
         for r in range(4):
             load_scales(1, r)
         identity = keep.tile([P, P], F32, name="identity")
@@ -268,7 +264,7 @@ def tile_fluxattention_pa_s_kernel(
         multiply(v_bank[0][:], 0, 2 * HD, HD)
         spread_gains(2, 4)
         count = len(halves)
-        copies = {3: (0, 0), 4: (0, 1), 6: (1, 0)}
+        copies = {2: (0, 0), 3: (0, 1), 5: (1, 0)}
         ahead = 2
         squared = 0
         for step in range(count + 2):

@@ -84,7 +84,7 @@ def tile_fluxattention_pa_s_kernel(
 
         for s in range(STREAMS):
             nc.sync.dma_start(out=x_sb[s][:], in_=x_dram[s][0])
-        nc.scalar.dma_start(out=rot[:], in_=image_rotary_emb.rearrange("(s p) i c -> p s (i c)", s=STREAMS))
+        nc.sync.dma_start(out=rot[:], in_=image_rotary_emb.rearrange("(s p) i c -> p s (i c)", s=STREAMS))
         for r in range(4):
             load_scales(0, r)
 

from contextlib import ExitStack

import concourse.mybir as mybir
from concourse.masks import make_identity

F32 = mybir.dt.float32
BF16 = mybir.dt.bfloat16
I32 = mybir.dt.int32
U32 = mybir.dt.uint32
U8 = mybir.dt.uint8
FP8X4 = mybir.dt.float8_e4m3fn_x4
FP4X4 = mybir.dt.float4_e2m1fn_x4
ACT = mybir.ActivationFunctionType
ALU = mybir.AluOpType

P = 128
DM = 512
H = 8
D = 64
HD = H * D
EPS = 1e-6
STREAMS = 2

HALF = HD // 2
HH = H // 2
TENSOR_ADDS = 3
VECTOR_ADDS_FROM = 6

FLOPS = 2 * STREAMS * P * DM * 3 * HD


def tile_fluxattention_pa_s_kernel(
    tc,
    hidden_states,
    encoder_hidden_states,
    image_rotary_emb,
    W_iqkv_words,
    W_iqkv_scales,
    W_eqkv_words,
    W_eqkv_scales,
    qn_scale,
    kn_scale,
    eqn_scale,
    ekn_scale,
    out_0,
    out_1,
    out_2,
):
    nc = tc.nc
    x_dram = (encoder_hidden_states, hidden_states)
    words_dram = (W_eqkv_words, W_iqkv_words)
    scales_dram = (W_eqkv_scales, W_iqkv_scales)
    gains_dram = ((eqn_scale, ekn_scale), (qn_scale, kn_scale))
    outs = (out_0, out_1, out_2)

    units = [(s, j) for s in range(STREAMS) for j in range(2)]
    halves = [(s, j, e) for s, j in units for e in range(2)]

    with ExitStack() as ctx:
        keep = ctx.enter_context(tc.tile_pool(name="keep", bufs=1))
        psum = ctx.enter_context(tc.psum_pool(name="psum", bufs=1))
        ctx.enter_context(tc.manual_schedule())

        gain_rows = keep.tile([P, 4 * D], BF16, name="gain_rows")
        nc.gpsimd.memset(gain_rows[:], 0.0)
        w_scales = [keep.tile([P, 3 * HD], U8, name="w_scales%d" % s, align_bytes=64) for s in range(STREAMS)]
        nc.vector.memset(w_scales[0][:].bitcast(I32), 0)
        eps = keep.tile([P, 1], F32, name="eps")
        nc.vector.memset(eps[:], EPS)
        ones = keep.tile([P, P], BF16, name="ones")
        nc.vector.memset(ones[:], 1.0)
        nc.vector.memset(w_scales[1][:].bitcast(I32), 0)

        x_sb = [keep.tile([P, DM], BF16, name="x_sb%d" % s) for s in range(STREAMS)]
        w_words = [keep.tile([P, 2 * 3 * HD], U8, name="w_words%d" % s, align_bytes=64) for s in range(STREAMS)]
        rot = keep.tile([P, STREAMS, 2 * D], BF16, name="rot")

        def load_scales(s, r):
            nc.sync.dma_start(out=w_scales[s][r:P:32, :].bitcast(I32), in_=scales_dram[s][0, r:16:4, :].bitcast(I32))

        def load_gain(queue, n):
            s, j = units[n]
            queue.dma_start(out=gain_rows[0:1, n * D : (n + 1) * D], in_=gains_dram[s][j].unsqueeze(0))

        for s in range(STREAMS):
            nc.sync.dma_start(out=x_sb[s][:], in_=x_dram[s][0])
        nc.sync.dma_start(out=rot[:], in_=image_rotary_emb.rearrange("(s p) i c -> p s (i c)", s=STREAMS))
        for r in range(4):
            load_scales(0, r)

        def load_words(s):
            nc.sync.dma_start(out=w_words[s][:].bitcast(I32), in_=words_dram[s][0].bitcast(I32))

        load_words(0)
        for n in range(len(units)):
            load_gain(nc.sync, n)
        load_words(1)
        for r in range(4):
            load_scales(1, r)
        identity = keep.tile([P, P], F32, name="identity")
        make_identity(nc, identity[:])

        warm = keep.tile([P, 1], F32, name="warm")
        nc.scalar.activation(out=warm[:], in_=eps[:], func=ACT.Abs_reciprocal_sqrt)

        xt0 = psum.tile([P, 2 * P], F32, name="xt0")
        shared = psum.tile([P, 4 * D + 2 * P], F32, name="shared")
        gain_all = shared[:, 0 : 4 * D]
        xt = [xt0[:].rearrange("p (u r) -> p u r", u=2), shared[:, 4 * D : 4 * D + 2 * P].rearrange("p (u r) -> p u r", u=2)]
        x_codes = []
        x_scales = []

        def transposes(s):
            for u in range(2):
                nc.tensor.transpose(xt[s][:, u, :], x_sb[s][:].bitcast(F32)[:, u : DM // 2 : 2], identity[:])

        def quantise(s):
            grouped = keep.tile([P, 4 * P], BF16, name="grouped%d" % s, align_bytes=64)
            nc.scalar.copy(
                out=grouped[:].bitcast(F32).rearrange("p (r u) -> p r u", u=2),
                in_=xt[s].rearrange("p u r -> p r u"),
            )
            codes = keep.tile([P, P], U32, name="x_codes%d" % s, align_bytes=64)
            scales = keep.tile([P, P], U8, name="x_scales%d" % s, align_bytes=64)
            nc.vector.quantize_mx(out=codes[:].bitcast(FP8X4), scales=scales[:], in_=grouped[:])
            x_codes.append(codes)
            x_scales.append(scales)

        def multiply(out, s, col, width):
            nc.tensor.matmul_mx(
                out=out,
                lhsT=x_codes[s][:].bitcast(FP8X4),
                lhsT_scale=x_scales[s][:],
                rhs=w_words[s][:, 2 * col : 2 * (col + width)].bitcast(FP4X4),
                rhs_scale=w_scales[s][:, col : col + width],
                start=True,
                stop=True,
            )

        qk = [psum.tile([P, HD], F32, name="qk%d" % b) for b in range(4)]
        v_bank = [psum.tile([P, HD], F32, name="v_bank%d" % s) for s in range(STREAMS)]

        def piece(m):
            s, j, e = halves[m]
            return qk[2 * j + e][:, s * HALF : (s + 1) * HALF]

        def project(m):
            s, j, e = halves[m]
            multiply(piece(m), s, j * HD + e * HALF, HALF)

        g = {}

        def fold_gain(n):
            s = units[n][0]
            cols = slice(n * D, (n + 1) * D)
            g[n] = keep.tile([P, 2 * D], F32, name="g%d" % n)
            nc.vector.tensor_tensor(
                out=g[n][:].rearrange("p (i b a) -> p i b a", a=2, b=2),
                in0=rot[:, s, :].rearrange("p (i a b) -> p i b a", a=2, b=2),
                in1=gain_all[:, cols].rearrange("p (i b) -> p i b", b=2).unsqueeze(3).to_broadcast([P, D // 2, 2, 2]),
                op=ALU.mult,
            )

        rstd = {}

        squares = {}
        sumsq = {}

        def square(m, h):
            if h == 0:
                squares[m] = keep.tile([P, HALF], F32, name="squares%d" % m)
                sumsq[m] = keep.tile([P, HH], F32, name="sumsq%d" % m)
            head = slice(h * D, (h + 1) * D)
            nc.scalar.activation(
                out=squares[m][:, head], in_=piece(m)[:, head], func=ACT.Square, accum_out=sumsq[m][:, h : h + 1]
            )

        def invert(m, first, last):
            if first == 0:
                rstd[m] = keep.tile([P, HH], F32, name="rstd%d" % m)
            nc.scalar.activation(
                out=rstd[m][:, first:last],
                in_=sumsq[m][:, first:last],
                func=ACT.Abs_reciprocal_sqrt,
                bias=eps[:],
                scale=1.0 / D,
            )

        term = {}

        def products(m):
            term[m] = keep.tile([P, 2 * HALF], F32, name="term%d" % m)
            for h in range(HH):
                nc.vector.scalar_tensor_tensor(
                    out=term[m][:, 2 * h * D : 2 * (h + 1) * D].rearrange("p (c a) -> p c a", a=2),
                    in0=piece(m)[:, h * D : (h + 1) * D].unsqueeze(2).to_broadcast([P, D, 2]),
                    scalar=rstd[m][:, h : h + 1],
                    in1=g[m // 2][:].rearrange("p (c a) -> p c a", a=2),
                    op0=ALU.mult,
                    op1=ALU.mult,
                )

        def both_terms(m):
            both = term[m][:].rearrange("p (c b a) -> p c b a", b=2, a=2)
            return [both[:, :, b, :] for b in range(2)]

        def add_and_store(engine, m):
            terms = both_terms(m)
            rotated = keep.tile([P, HALF], F32, name="rotated%d" % m)
            engine.tensor_tensor(
                out=rotated[:].rearrange("p (c a) -> p c a", a=2), in0=terms[0], in1=terms[1], op=ALU.add
            )
            store(m, rotated)

        tensor_sum = v_bank[0][:, 0:HALF]

        def add_on_tensor(m):
            for b, one_term in enumerate(both_terms(m)):
                nc.tensor.matmul(
                    tensor_sum.rearrange("p (c a) -> p c a", a=2),
                    lhsT=identity[:],
                    rhs=one_term,
                    start=b == 0,
                    stop=b == 1,
                )

        def copy_and_store(m):
            rotated = keep.tile([P, HALF], F32, name="rotated%d" % m)
            nc.scalar.copy(out=rotated[:], in_=tensor_sum)
            store(m, rotated)

        def store(m, rotated):
            s, j, e = halves[m]
            nc.sync.dma_start(out=outs[j][0, s * P : (s + 1) * P, e * HALF : (e + 1) * HALF], in_=rotated[:])

        v_sb = {}

        def copy_v(s, e):
            if e == 0:
                v_sb[s] = keep.tile([P, HD], F32, name="v_sb%d" % s)
            cols = slice(e * HALF, (e + 1) * HALF)
            nc.scalar.copy(out=v_sb[s][:, cols], in_=v_bank[s][:, cols])
            first = 0 if s == 0 else e * HALF
            if s == 1 or e == 1:
                nc.sync.dma_start(
                    out=outs[2][0, s * P : (s + 1) * P, first : (e + 1) * HALF], in_=v_sb[s][:, first : (e + 1) * HALF]
                )

        def spread_gains(first, last):
            cols = slice(first * D, last * D)
            nc.tensor.matmul(gain_all[:, cols], lhsT=ones[:], rhs=gain_rows[:, cols], start=True, stop=True)

        transposes(0)
        quantise(0)
        transposes(1)
        quantise(1)
        for m in range(2):
            project(m)
        spread_gains(0, 2)
        for n in range(2):
            fold_gain(n)
        for m in range(2, 4):
            project(m)
        multiply(v_bank[0][:], 0, 2 * HD, HD)
        spread_gains(2, 4)
        count = len(halves)
        copies = {2: (0, 0), 3: (0, 1), 5: (1, 0)}
        ahead = 2
        squared = 0
        for step in range(count + 2):
            if step < count:
                for h in range(squared, HH):
                    square(step, h)
                squared = 0
                inverted = 0
                if step == 0:
                    inverted = HH // 2
                    invert(0, 0, inverted)
                if step in copies:
                    copy_v(*copies[step])
                elif step + 1 < count:
                    for h in range(ahead):
                        square(step + 1, h)
                    squared = ahead
                invert(step, inverted, HH)
                if step == count - 1:
                    copy_v(1, 1)
                    copy_and_store(TENSOR_ADDS)
            if 1 <= step <= count:
                m = step - 1
                products(m)
                if m == 1:
                    for n in range(2, len(units)):
                        fold_gain(n)
                if m + 4 < count:
                    project(m + 4)
                if m == 1:
                    multiply(v_bank[1][:], 1, 2 * HD, HD)
                if m == TENSOR_ADDS:
                    add_on_tensor(m)
            if 2 <= step < VECTOR_ADDS_FROM + 2 and step - 2 != TENSOR_ADDS:
                add_and_store(nc.gpsimd, step - 2)
        for m in range(VECTOR_ADDS_FROM, count):
            add_and_store(nc.vector, m)
